import numpy as np
import ml_dtypes


def mxq(x, axis, fmt="e4m3"):
    dtype, down = {"e4m3": (ml_dtypes.float8_e4m3fn, 7), "e5m2": (ml_dtypes.float8_e5m2, 14)}[fmt]
    v = np.moveaxis(np.asarray(x, np.float32).astype(ml_dtypes.bfloat16).astype(np.float64), axis, -1)
    blocks = v.reshape(v.shape[:-1] + (-1, 32))
    amax = np.abs(blocks).max(-1, keepdims=True)
    byte = np.maximum(np.where(amax > 0, np.frexp(amax)[1] - 1 + 127, 0) - down, 1)
    scale = np.exp2(byte - 127.0)
    codes = (blocks / scale).astype(np.float32).astype(dtype).astype(np.float64)
    return np.moveaxis((codes * scale).reshape(v.shape), -1, axis)


WIDE = False


def mx_kscale(k):
    if not WIDE:
        return np.ones(k)
    levels = np.array([20, -20, 10, -10, 0])
    a = np.random.permutation(np.resize(levels, k // 512 * 4)).reshape(k // 512, 4)
    idx = np.arange(k)
    return np.exp2(a[idx // 512, idx % 128 // 32])


BF16 = ml_dtypes.bfloat16


def bf(x):
    return np.asarray(x, np.float32).astype(BF16)


def f64(x):
    return np.asarray(x).astype(np.float64)


B, I, O, NK, ORDER = 1024, 512, 512, 16, 3
K = NK - ORDER


def silu(v):
    return v / (1.0 + np.exp(-v))


def make_knots():
    return np.linspace(-1.0 - 2.0 / NK, 1.0 + 2.0 / NK, NK)


def bspline_bases(t, knots, order):
    tb = t[:, None]
    b = ((knots[:-1] <= tb) & (knots[1:] > tb)).astype(np.float64)
    for k in range(1, order):
        left = (tb - knots[:-k - 1]) / (knots[k:-1] - knots[:-k - 1]) * b[:, :-1]
        right = (knots[k + 1:] - tb) / (knots[k + 1:] - knots[1:-k]) * b[:, 1:]
        b = left + right
    return b


def setup_inputs():
    s = mx_kscale(B)
    sb = np.repeat(s.reshape(-1, 32)[:, 0], 32)
    loud = sb >= max(2.0, sb.max() / 4.0)
    x = np.random.uniform(-1.0, 1.0, (B, I))
    x[loud] = -80.0 + 16.0 * x[loud]
    p = np.random.standard_normal((O, I, K)) * 1.5 / np.sqrt(I)
    w_b = (1.0 + 0.1 * np.random.standard_normal(1)) / np.sqrt(I)
    w_s = 1.0 + 0.1 * np.random.standard_normal(1)
    g = np.random.standard_normal((B, O)) * np.exp2(np.random.randint(-12, 1, (B, 1)))
    g = np.where(loud[:, None], g * (sb * sb)[:, None], g)
    return {"x": bf(x),
            "spline_parameters": bf(p),
            "w_b": bf(w_b),
            "w_s": bf(w_s),
            "grad_out": bf(g)}


def reference(x, spline_parameters, w_b, w_s, grad_out):
    x = f64(x)
    bases = bspline_bases(x.reshape(-1), make_knots(), ORDER)
    bases = bases.reshape(B, I * K)
    d = mxq(f64(grad_out), 0, "e5m2").T @ mxq(bases, 0, "e4m3")
    return f64(w_s) * d.reshape(O, I, K)

@@ -1,0 +1,218 @@
+import math
+from contextlib import ExitStack
+
+import concourse.mybir as mybir
+
+BF16 = mybir.dt.bfloat16
+F32 = mybir.dt.float32
+I32 = mybir.dt.int32
+U32 = mybir.dt.uint32
+U8 = mybir.dt.uint8
+E4X4 = mybir.dt.float8_e4m3fn_x4
+E5X4 = mybir.dt.float8_e5m2_x4
+ALU = mybir.AluOpType
+ACT = mybir.ActivationFunctionType
+
+P = 128
+PACK = 4
+TOKENS, FEATURES, OUTS, BASES = 1024, 512, 512, 13
+PASSES = TOKENS // (P * PACK)
+N_MOVING = 512
+GROUPS = 2
+CHUNK_FEATURES = [38,38,38,38,38,38,28]
+SLAB = N_MOVING * PACK
+LANES = PASSES * GROUPS
+MANUAL = False
+AHEAD = 2
+
+FLOPS = 2 * TOKENS * OUTS * FEATURES * BASES
+BYTES = 2 * TOKENS * FEATURES * 2 + 2 + OUTS * FEATURES * BASES * 4
+
+STEP = 0.15
+ROOT2 = math.sqrt(2.0)
+SHIFT = 8.0
+
+
+def tile_bsplinekanlayer_kernel(tc, x, spline_parameters, w_b, w_s, grad_out, out):
+    nc = tc.nc
+    starts = [GROUPS * sum(CHUNK_FEATURES[:n]) for n in range(len(CHUNK_FEATURES))]
+    assert GROUPS * sum(CHUNK_FEATURES) == FEATURES
+    with ExitStack() as ctx:
+        if MANUAL:
+            ctx.enter_context(tc.manual_schedule())
+        keep = ctx.enter_context(tc.tile_pool(name="keep", bufs=1))
+        two = ctx.enter_context(tc.tile_pool(name="two", bufs=2))
+        three = ctx.enter_context(tc.tile_pool(name="three", bufs=3))
+        four = ctx.enter_context(tc.tile_pool(name="four", bufs=4))
+        outp = ctx.enter_context(tc.tile_pool(name="outp", bufs=6))
+        psum = ctx.enter_context(tc.psum_pool(name="psum", bufs=8))
+
+        x_raw = keep.tile([P, PASSES, PACK, FEATURES], BF16)
+        nc.sync.dma_start(out=x_raw[:], in_=x.rearrange("(c p j) i -> p c j i", c=PASSES, p=P, j=PACK))
+        g_raw = keep.tile([P, PASSES, PACK, OUTS], BF16)
+        nc.scalar.dma_start(out=g_raw[:], in_=grad_out.rearrange("(c p j) o -> p c j o", c=PASSES, p=P, j=PACK))
+        ws_bf = keep.tile([P, 1], BF16)
+        nc.sync.dma_start(out=ws_bf[:], in_=w_s.partition_broadcast(P))
+
+        slabs = []
+        for n in range(2):
+            slab = keep.tile([P, LANES, SLAB], BF16, name="slab%d" % n, align_bytes=64)
+            nc.vector.memset(slab[:, :, BASES * PACK * max(CHUNK_FEATURES) : SLAB], 0.0)
+            slabs.append(slab)
+        ws = keep.tile([P, 1], F32)
+        nc.vector.tensor_copy(out=ws[:], in_=ws_bf[:])
+
+        g_grouped = keep.tile([P, PASSES, OUTS, PACK], BF16, align_bytes=64)
+        g_codes = keep.tile([P, PASSES, OUTS], U32, align_bytes=64)
+        g_scales = keep.tile([P, PASSES, OUTS], U8, align_bytes=64)
+
+        state = {}
+
+        def stage_a(ch):
+            ni = CHUNK_FEATURES[ch]
+            size = LANES * ni * PACK
+            xg = two.tile([P, size], BF16, tag="xg")
+            nc.vector.tensor_scalar(
+                out=xg[:].rearrange("p (c i j) -> p c i j", c=PASSES, j=PACK),
+                in0=x_raw[:, :, :, starts[ch] : starts[ch] + GROUPS * ni].rearrange("p c j i -> p c i j"),
+                scalar1=-2.0,
+                scalar2=2.0,
+                op0=ALU.max,
+                op1=ALU.min,
+            )
+            si0 = two.tile([P, size], I32, tag="si0")
+            nc.vector.tensor_scalar(out=si0[:], in0=xg[:], scalar1=1.0 / (3.0 * STEP), scalar2=None, op0=ALU.mult)
+            si1 = two.tile([P, size], I32, tag="si1")
+            nc.vector.tensor_scalar(
+                out=si1[:], in0=xg[:], scalar1=1.0 / (3.0 * STEP), scalar2=SHIFT - 1.0 / 3.0, op0=ALU.mult, op1=ALU.add
+            )
+            si2 = two.tile([P, size], I32, tag="si2")
+            nc.vector.tensor_scalar(
+                out=si2[:], in0=xg[:], scalar1=1.0 / (3.0 * STEP), scalar2=SHIFT - 2.0 / 3.0, op0=ALU.mult, op1=ALU.add
+            )
+            sb0 = four.tile([P, size], BF16, tag="sb0")
+            nc.vector.tensor_scalar(out=sb0[:], in0=si0[:], scalar1=3.0, scalar2=None, op0=ALU.mult)
+            z = two.tile([P, size], F32, tag="z")
+            nc.vector.scalar_tensor_tensor(
+                out=z[:], in0=xg[:], scalar=1.0 / STEP, in1=sb0[:], op0=ALU.mult, op1=ALU.subtract
+            )
+            state[ch] = {"si1": si1, "si2": si2, "sb0": sb0, "z": z, "size": size}
+
+        def stage_b(ch):
+            st = state[ch]
+            size = st["size"]
+            z = st["z"]
+            dist = two.tile([P, size], F32, tag="dist")
+            nc.scalar.activation(out=dist[:], in_=z[:], func=ACT.Abs)
+            fold = two.tile([P, size], F32, tag="fold")
+            nc.scalar.activation(out=fold[:], in_=dist[:], func=ACT.Abs, bias=-0.5, scale=1.0)
+            dip = two.tile([P, size], F32, tag="dip")
+            nc.scalar.activation(out=dip[:], in_=fold[:], func=ACT.Square, bias=-ROOT2 / 2.0, scale=ROOT2)
+            cap = three.tile([P, size], BF16, tag="cap")
+            nc.scalar.activation(out=cap[:], in_=dip[:], func=ACT.Identity, bias=1.5, scale=-1.0)
+            env0 = three.tile([P, size], BF16, tag="env0")
+            nc.scalar.activation(out=env0[:], in_=dist[:], func=ACT.Square, bias=1.5, scale=-1.0)
+            env1 = three.tile([P, size], BF16, tag="env1")
+            nc.scalar.activation(out=env1[:], in_=z[:], func=ACT.Square, bias=0.5, scale=1.0)
+            env2 = three.tile([P, size], BF16, tag="env2")
+            nc.scalar.activation(out=env2[:], in_=z[:], func=ACT.Square, bias=-0.5, scale=1.0)
+            sb1 = four.tile([P, size], BF16, tag="sb1")
+            nc.scalar.copy(out=sb1[:], in_=st["si1"][:].bitcast(U32))
+            sb2 = four.tile([P, size], BF16, tag="sb2")
+            nc.scalar.copy(out=sb2[:], in_=st["si2"][:].bitcast(U32))
+            st["env"] = (env0, env1, env2)
+            st["cap"] = cap
+            st["sb"] = (st["sb0"], sb1, sb2)
+
+        def stage_x(ch):
+            st = state[ch]
+            size = st["size"]
+            plane = size // LANES
+            slab = slabs[ch % 2]
+            planes = slab[:, :, 0 : BASES * plane].rearrange("p a (k e) -> p k a e", k=BASES)
+            vals = []
+            for r in range(3):
+                val = two.tile([P, size], BF16, name="val%d" % r, tag="val%d" % r)
+                nc.vector.tensor_tensor(out=val[:], in0=st["env"][r][:], in1=st["cap"][:], op=ALU.min)
+                vals.append(val)
+            for r in range(3):
+                slots = len(range(r, BASES, 3))
+                mask = three.tile([P, slots, size], BF16, tag="mask")
+                for m in range(slots):
+                    wanted = 3.0 * (m - 2) if r == 0 else m - 2 + SHIFT
+                    nc.vector.tensor_scalar(
+                        out=mask[:, m, :], in0=st["sb"][r][:], scalar1=wanted, scalar2=0.5, op0=ALU.is_equal, op1=ALU.mult
+                    )
+                nc.vector.tensor_tensor(
+                    out=planes[:, r:BASES:3, :, :],
+                    in0=mask[:].rearrange("p m (a e) -> p m a e", a=LANES),
+                    in1=vals[r][:].rearrange("p (a e) -> p a e", a=LANES).unsqueeze(1).to_broadcast([P, slots, LANES, plane]),
+                    op=ALU.mult,
+                )
+
+        def stage_q(ch):
+            slab = slabs[ch % 2]
+            codes = three.tile([P, PASSES, GROUPS * N_MOVING], U32, tag="codes", align_bytes=64)
+            scales = three.tile([P, PASSES, GROUPS * N_MOVING], U8, tag="scales", align_bytes=64)
+            for c in range(PASSES):
+                nc.vector.quantize_mx(
+                    out=codes[:, c, :].bitcast(E4X4),
+                    scales=scales[:, c, :],
+                    in_=slab[:, c * GROUPS : (c + 1) * GROUPS, :].rearrange("p a e -> p (a e)"),
+                )
+            state[ch]["codes"] = codes
+            state[ch]["scales"] = scales
+
+        def stage_out(ch):
+            ni = CHUNK_FEATURES[ch]
+            codes = state[ch]["codes"]
+            scales = state[ch]["scales"]
+            width = ni * BASES
+            for ot in range(OUTS // P):
+                rows = slice(ot * P, (ot + 1) * P)
+                stage = outp.tile([P, GROUPS * width], F32, tag="stage")
+                for g in range(GROUPS):
+                    cols = slice(g * N_MOVING, (g + 1) * N_MOVING)
+                    acc = psum.tile([P, N_MOVING], F32, tag="acc")
+                    for c in range(PASSES):
+                        nc.tensor.matmul_mx(
+                            out=acc[:],
+                            lhsT=g_codes[:, c, rows].bitcast(E5X4),
+                            lhsT_scale=g_scales[:, c, rows],
+                            rhs=codes[:, c, cols].bitcast(E4X4),
+                            rhs_scale=scales[:, c, cols],
+                            start=(c == 0),
+                            stop=(c == PASSES - 1),
+                        )
+                    nc.scalar.activation(
+                        out=stage[:, g * width : (g + 1) * width].rearrange("p (i k) -> p i k", k=BASES),
+                        in_=acc[:, 0:width].rearrange("p (k i) -> p i k", k=BASES),
+                        func=ACT.Copy,
+                        scale=ws[:, 0:1],
+                    )
+                nc.sync.dma_start(
+                    out=out[rows, starts[ch] : starts[ch] + GROUPS * ni, :].rearrange("o i k -> o (i k)"),
+                    in_=stage[:],
+                )
+
+        n_chunks = len(CHUNK_FEATURES)
+        stage_a(0)
+        stage_b(0)
+        for c in range(PASSES):
+            nc.scalar.copy(out=g_grouped[:, c], in_=g_raw[:, c].rearrange("p j o -> p o j"))
+        for ch in range(1, AHEAD):
+            stage_a(ch)
+            stage_b(ch)
+        for c in range(PASSES):
+            nc.vector.quantize_mx(
+                out=g_codes[:, c, :].bitcast(E5X4),
+                scales=g_scales[:, c, :],
+                in_=g_grouped[:, c].rearrange("p o j -> p (o j)"),
+            )
+        for ch in range(n_chunks):
+            stage_x(ch)
+            if ch + AHEAD < n_chunks:
+                stage_a(ch + AHEAD)
+                stage_b(ch + AHEAD)
+            stage_q(ch)
+            stage_out(ch)

@@ -18,11 +18,12 @@ PACK = 4
 TOKENS, FEATURES, OUTS, BASES = 1024, 512, 512, 13
 PASSES = TOKENS // (P * PACK)
 N_MOVING = 512
-GROUPS = 2
-CHUNK_FEATURES = [38,38,38,38,38,38,28]
+MAX_GROUPS = 2
+CHUNKS = [(2, 38), (2, 38), (2, 38), (2, 38), (2, 38), (2, 28), (1, 38), (1, 38)]
 SLAB = N_MOVING * PACK
-LANES = PASSES * GROUPS
 MANUAL = False
+ACT_CASTS = 2
+X_SPLIT = 160
 AHEAD = 2
 
 FLOPS = 2 * TOKENS * OUTS * FEATURES * BASES
@@ -35,8 +36,9 @@ SHIFT = 8.0
 
 def tile_bsplinekanlayer_kernel(tc, x, spline_parameters, w_b, w_s, grad_out, out):
     nc = tc.nc
-    starts = [GROUPS * sum(CHUNK_FEATURES[:n]) for n in range(len(CHUNK_FEATURES))]
-    assert GROUPS * sum(CHUNK_FEATURES) == FEATURES
+    spans = [groups * ni for groups, ni in CHUNKS]
+    starts = [sum(spans[:n]) for n in range(len(CHUNKS))]
+    assert sum(spans) == FEATURES
     with ExitStack() as ctx:
         if MANUAL:
             ctx.enter_context(tc.manual_schedule())
@@ -48,16 +50,19 @@ def tile_bsplinekanlayer_kernel(tc, x, spline_parameters, w_b, w_s, grad_out, ou
         psum = ctx.enter_context(tc.psum_pool(name="psum", bufs=8))
 
         x_raw = keep.tile([P, PASSES, PACK, FEATURES], BF16)
-        nc.sync.dma_start(out=x_raw[:], in_=x.rearrange("(c p j) i -> p c j i", c=PASSES, p=P, j=PACK))
+        x_view = x.rearrange("(c p j) i -> p c j i", c=PASSES, p=P, j=PACK)
+        for piece in (slice(0, X_SPLIT), slice(X_SPLIT, FEATURES)):
+            for c in range(PASSES):
+                nc.sync.dma_start(out=x_raw[:, c, :, piece], in_=x_view[:, c, :, piece])
         g_raw = keep.tile([P, PASSES, PACK, OUTS], BF16)
-        nc.scalar.dma_start(out=g_raw[:], in_=grad_out.rearrange("(c p j) o -> p c j o", c=PASSES, p=P, j=PACK))
+        nc.sync.dma_start(out=g_raw[:], in_=grad_out.rearrange("(c p j) o -> p c j o", c=PASSES, p=P, j=PACK))
         ws_bf = keep.tile([P, 1], BF16)
         nc.sync.dma_start(out=ws_bf[:], in_=w_s.partition_broadcast(P))
 
         slabs = []
         for n in range(2):
-            slab = keep.tile([P, LANES, SLAB], BF16, name="slab%d" % n, align_bytes=64)
-            nc.vector.memset(slab[:, :, BASES * PACK * max(CHUNK_FEATURES) : SLAB], 0.0)
+            slab = keep.tile([P, PASSES * MAX_GROUPS, SLAB], BF16, name="slab%d" % n, align_bytes=64)
+            nc.vector.memset(slab[:, :, BASES * PACK * max(ni for groups, ni in CHUNKS) : SLAB], 0.0)
             slabs.append(slab)
         ws = keep.tile([P, 1], F32)
         nc.vector.tensor_copy(out=ws[:], in_=ws_bf[:])
@@ -69,12 +74,12 @@ def tile_bsplinekanlayer_kernel(tc, x, spline_parameters, w_b, w_s, grad_out, ou
         state = {}
 
         def stage_a(ch):
-            ni = CHUNK_FEATURES[ch]
-            size = LANES * ni * PACK
+            groups, ni = CHUNKS[ch]
+            size = PASSES * groups * ni * PACK
             xg = two.tile([P, size], BF16, tag="xg")
             nc.vector.tensor_scalar(
                 out=xg[:].rearrange("p (c i j) -> p c i j", c=PASSES, j=PACK),
-                in0=x_raw[:, :, :, starts[ch] : starts[ch] + GROUPS * ni].rearrange("p c j i -> p c i j"),
+                in0=x_raw[:, :, :, starts[ch] : starts[ch] + spans[ch]].rearrange("p c j i -> p c i j"),
                 scalar1=-2.0,
                 scalar2=2.0,
                 op0=ALU.max,
@@ -82,21 +87,22 @@ def tile_bsplinekanlayer_kernel(tc, x, spline_parameters, w_b, w_s, grad_out, ou
             )
             si0 = two.tile([P, size], I32, tag="si0")
             nc.vector.tensor_scalar(out=si0[:], in0=xg[:], scalar1=1.0 / (3.0 * STEP), scalar2=None, op0=ALU.mult)
-            si1 = two.tile([P, size], I32, tag="si1")
-            nc.vector.tensor_scalar(
-                out=si1[:], in0=xg[:], scalar1=1.0 / (3.0 * STEP), scalar2=SHIFT - 1.0 / 3.0, op0=ALU.mult, op1=ALU.add
-            )
-            si2 = two.tile([P, size], I32, tag="si2")
-            nc.vector.tensor_scalar(
-                out=si2[:], in0=xg[:], scalar1=1.0 / (3.0 * STEP), scalar2=SHIFT - 2.0 / 3.0, op0=ALU.mult, op1=ALU.add
-            )
+            sis = [None]
+            for r in (1, 2):
+                si = two.tile([P, size], U32, name="si%d" % r, tag="si%d" % r)
+                if r > ACT_CASTS:
+                    nc.vector.tensor_scalar(
+                        out=si[:].bitcast(I32), in0=xg[:], scalar1=1.0 / (3.0 * STEP), scalar2=SHIFT - r / 3.0,
+                        op0=ALU.mult, op1=ALU.add,
+                    )
+                sis.append(si)
             sb0 = four.tile([P, size], BF16, tag="sb0")
             nc.vector.tensor_scalar(out=sb0[:], in0=si0[:], scalar1=3.0, scalar2=None, op0=ALU.mult)
             z = two.tile([P, size], F32, tag="z")
             nc.vector.scalar_tensor_tensor(
                 out=z[:], in0=xg[:], scalar=1.0 / STEP, in1=sb0[:], op0=ALU.mult, op1=ALU.subtract
             )
-            state[ch] = {"si1": si1, "si2": si2, "sb0": sb0, "z": z, "size": size}
+            state[ch] = {"si": sis, "xg": xg, "sb0": sb0, "z": z, "size": size}
 
         def stage_b(ch):
             st = state[ch]
@@ -116,20 +122,26 @@ def tile_bsplinekanlayer_kernel(tc, x, spline_parameters, w_b, w_s, grad_out, ou
             nc.scalar.activation(out=env1[:], in_=z[:], func=ACT.Square, bias=0.5, scale=1.0)
             env2 = three.tile([P, size], BF16, tag="env2")
             nc.scalar.activation(out=env2[:], in_=z[:], func=ACT.Square, bias=-0.5, scale=1.0)
-            sb1 = four.tile([P, size], BF16, tag="sb1")
-            nc.scalar.copy(out=sb1[:], in_=st["si1"][:].bitcast(U32))
-            sb2 = four.tile([P, size], BF16, tag="sb2")
-            nc.scalar.copy(out=sb2[:], in_=st["si2"][:].bitcast(U32))
+            sbs = [st["sb0"]]
+            for r in (1, 2):
+                if r <= ACT_CASTS:
+                    nc.scalar.activation(
+                        out=st["si"][r][:], in_=st["xg"][:], func=ACT.Identity, bias=SHIFT - r / 3.0, scale=1.0 / (3.0 * STEP)
+                    )
+                sb = four.tile([P, size], BF16, name="sb%d" % r, tag="sb%d" % r)
+                nc.scalar.copy(out=sb[:], in_=st["si"][r][:])
+                sbs.append(sb)
             st["env"] = (env0, env1, env2)
             st["cap"] = cap
-            st["sb"] = (st["sb0"], sb1, sb2)
+            st["sb"] = sbs
 
         def stage_x(ch):
             st = state[ch]
             size = st["size"]
-            plane = size // LANES
+            lanes = PASSES * CHUNKS[ch][0]
+            plane = size // lanes
             slab = slabs[ch % 2]
-            planes = slab[:, :, 0 : BASES * plane].rearrange("p a (k e) -> p k a e", k=BASES)
+            planes = slab[:, 0:lanes, 0 : BASES * plane].rearrange("p a (k e) -> p k a e", k=BASES)
             vals = []
             for r in range(3):
                 val = two.tile([P, size], BF16, name="val%d" % r, tag="val%d" % r)
@@ -145,33 +157,34 @@ def tile_bsplinekanlayer_kernel(tc, x, spline_parameters, w_b, w_s, grad_out, ou
                     )
                 nc.vector.tensor_tensor(
                     out=planes[:, r:BASES:3, :, :],
-                    in0=mask[:].rearrange("p m (a e) -> p m a e", a=LANES),
-                    in1=vals[r][:].rearrange("p (a e) -> p a e", a=LANES).unsqueeze(1).to_broadcast([P, slots, LANES, plane]),
+                    in0=mask[:].rearrange("p m (a e) -> p m a e", a=lanes),
+                    in1=vals[r][:].rearrange("p (a e) -> p a e", a=lanes).unsqueeze(1).to_broadcast([P, slots, lanes, plane]),
                     op=ALU.mult,
                 )
 
         def stage_q(ch):
             slab = slabs[ch % 2]
-            codes = three.tile([P, PASSES, GROUPS * N_MOVING], U32, tag="codes", align_bytes=64)
-            scales = three.tile([P, PASSES, GROUPS * N_MOVING], U8, tag="scales", align_bytes=64)
+            groups = CHUNKS[ch][0]
+            codes = three.tile([P, PASSES, groups * N_MOVING], U32, tag="codes", align_bytes=64)
+            scales = three.tile([P, PASSES, groups * N_MOVING], U8, tag="scales", align_bytes=64)
             for c in range(PASSES):
                 nc.vector.quantize_mx(
                     out=codes[:, c, :].bitcast(E4X4),
                     scales=scales[:, c, :],
-                    in_=slab[:, c * GROUPS : (c + 1) * GROUPS, :].rearrange("p a e -> p (a e)"),
+                    in_=slab[:, c * groups : (c + 1) * groups, :].rearrange("p a e -> p (a e)"),
                 )
             state[ch]["codes"] = codes
             state[ch]["scales"] = scales
 
         def stage_out(ch):
-            ni = CHUNK_FEATURES[ch]
+            groups, ni = CHUNKS[ch]
             codes = state[ch]["codes"]
             scales = state[ch]["scales"]
             width = ni * BASES
             for ot in range(OUTS // P):
                 rows = slice(ot * P, (ot + 1) * P)
-                stage = outp.tile([P, GROUPS * width], F32, tag="stage")
-                for g in range(GROUPS):
+                stage = outp.tile([P, groups * width], F32, tag="stage")
+                for g in range(groups):
                     cols = slice(g * N_MOVING, (g + 1) * N_MOVING)
                     acc = psum.tile([P, N_MOVING], F32, tag="acc")
                     for c in range(PASSES):
@@ -191,11 +204,11 @@ def tile_bsplinekanlayer_kernel(tc, x, spline_parameters, w_b, w_s, grad_out, ou
                         scale=ws[:, 0:1],
                     )
                 nc.sync.dma_start(
-                    out=out[rows, starts[ch] : starts[ch] + GROUPS * ni, :].rearrange("o i k -> o (i k)"),
+                    out=out[rows, starts[ch] : starts[ch] + spans[ch], :].rearrange("o i k -> o (i k)"),
                     in_=stage[:],
                 )
 
-        n_chunks = len(CHUNK_FEATURES)
+        n_chunks = len(CHUNKS)
         stage_a(0)
         stage_b(0)
         for c in range(PASSES):

@@ -19,12 +19,12 @@ TOKENS, FEATURES, OUTS, BASES = 1024, 512, 512, 13
 PASSES = TOKENS // (P * PACK)
 N_MOVING = 512
 MAX_GROUPS = 2
-CHUNKS = [(2, 38), (2, 38), (2, 38), (2, 38), (2, 38), (2, 28), (1, 38), (1, 38)]
+CHUNKS = [(1, 38), (1, 38), (2, 38), (2, 38), (2, 38), (2, 38), (2, 28), (1, 38), (1, 38)]
 SLAB = N_MOVING * PACK
 MANUAL = False
 ACT_CASTS = 2
 X_SPLIT = 160
-AHEAD = 2
+AHEAD = 3
 
 FLOPS = 2 * TOKENS * OUTS * FEATURES * BASES
 BYTES = 2 * TOKENS * FEATURES * 2 + 2 + OUTS * FEATURES * BASES * 4
@@ -181,15 +181,17 @@ def tile_bsplinekanlayer_kernel(tc, x, spline_parameters, w_b, w_s, grad_out, ou
             codes = state[ch]["codes"]
             scales = state[ch]["scales"]
             width = ni * BASES
-            for ot in range(OUTS // P):
-                rows = slice(ot * P, (ot + 1) * P)
-                stage = outp.tile([P, groups * width], F32, tag="stage")
-                for g in range(groups):
-                    cols = slice(g * N_MOVING, (g + 1) * N_MOVING)
-                    acc = psum.tile([P, N_MOVING], F32, tag="acc")
-                    for c in range(PASSES):
+            accs = {}
+            for c in range(PASSES):
+                for ot in range(OUTS // P):
+                    rows = slice(ot * P, (ot + 1) * P)
+                    for g in range(groups):
+                        cols = slice(g * N_MOVING, (g + 1) * N_MOVING)
+                        if c == 0:
+                            acc = psum.tile([P, N_MOVING], F32, tag="acc")
+                            accs[(ot, g)] = acc
                         nc.tensor.matmul_mx(
-                            out=acc[:],
+                            out=accs[(ot, g)][:],
                             lhsT=g_codes[:, c, rows].bitcast(E5X4),
                             lhsT_scale=g_scales[:, c, rows],
                             rhs=codes[:, c, cols].bitcast(E4X4),
@@ -197,6 +199,11 @@ def tile_bsplinekanlayer_kernel(tc, x, spline_parameters, w_b, w_s, grad_out, ou
                             start=(c == 0),
                             stop=(c == PASSES - 1),
                         )
+            for ot in range(OUTS // P):
+                rows = slice(ot * P, (ot + 1) * P)
+                stage = outp.tile([P, groups * width], F32, tag="stage")
+                for g in range(groups):
+                    acc = accs[(ot, g)]
                     nc.scalar.activation(
                         out=stage[:, g * width : (g + 1) * width].rearrange("p (i k) -> p i k", k=BASES),
                         in_=acc[:, 0:width].rearrange("p (k i) -> p i k", k=BASES),

@@ -18,13 +18,15 @@ PACK = 4
 TOKENS, FEATURES, OUTS, BASES = 1024, 512, 512, 13
 PASSES = TOKENS // (P * PACK)
 N_MOVING = 512
-MAX_GROUPS = 2
-CHUNKS = [(1, 38), (1, 38), (2, 38), (2, 38), (2, 38), (2, 38), (2, 28), (1, 38), (1, 38)]
+CHUNKS = [(2, 38), (2, 38), (2, 38), (2, 38), (2, 38), (2, 28), (1, 38), (1, 38)]
+MAX_GROUPS = max(groups for groups, ni in CHUNKS)
 SLAB = N_MOVING * PACK
-MANUAL = False
-ACT_CASTS = 2
+WIDEST = 4096
+ACT_CASTS = 1
 X_SPLIT = 160
-AHEAD = 3
+SLABS = 2
+AHEAD = 2
+DEEP = AHEAD + 1
 
 FLOPS = 2 * TOKENS * OUTS * FEATURES * BASES
 BYTES = 2 * TOKENS * FEATURES * 2 + 2 + OUTS * FEATURES * BASES * 4
@@ -40,12 +42,10 @@ def tile_bsplinekanlayer_kernel(tc, x, spline_parameters, w_b, w_s, grad_out, ou
     starts = [sum(spans[:n]) for n in range(len(CHUNKS))]
     assert sum(spans) == FEATURES
     with ExitStack() as ctx:
-        if MANUAL:
-            ctx.enter_context(tc.manual_schedule())
         keep = ctx.enter_context(tc.tile_pool(name="keep", bufs=1))
+        one = ctx.enter_context(tc.tile_pool(name="one", bufs=1))
         two = ctx.enter_context(tc.tile_pool(name="two", bufs=2))
-        three = ctx.enter_context(tc.tile_pool(name="three", bufs=3))
-        four = ctx.enter_context(tc.tile_pool(name="four", bufs=4))
+        deep = ctx.enter_context(tc.tile_pool(name="deep", bufs=DEEP))
         outp = ctx.enter_context(tc.tile_pool(name="outp", bufs=6))
         psum = ctx.enter_context(tc.psum_pool(name="psum", bufs=8))
 
@@ -60,7 +60,7 @@ def tile_bsplinekanlayer_kernel(tc, x, spline_parameters, w_b, w_s, grad_out, ou
         nc.sync.dma_start(out=ws_bf[:], in_=w_s.partition_broadcast(P))
 
         slabs = []
-        for n in range(2):
+        for n in range(SLABS):
             slab = keep.tile([P, PASSES * MAX_GROUPS, SLAB], BF16, name="slab%d" % n, align_bytes=64)
             nc.vector.memset(slab[:, :, BASES * PACK * max(ni for groups, ni in CHUNKS) : SLAB], 0.0)
             slabs.append(slab)
@@ -87,92 +87,77 @@ def tile_bsplinekanlayer_kernel(tc, x, spline_parameters, w_b, w_s, grad_out, ou
             )
             si0 = two.tile([P, size], I32, tag="si0")
             nc.vector.tensor_scalar(out=si0[:], in0=xg[:], scalar1=1.0 / (3.0 * STEP), scalar2=None, op0=ALU.mult)
-            sis = [None]
-            for r in (1, 2):
-                si = two.tile([P, size], U32, name="si%d" % r, tag="si%d" % r)
-                if r > ACT_CASTS:
-                    nc.vector.tensor_scalar(
-                        out=si[:].bitcast(I32), in0=xg[:], scalar1=1.0 / (3.0 * STEP), scalar2=SHIFT - r / 3.0,
-                        op0=ALU.mult, op1=ALU.add,
-                    )
-                sis.append(si)
-            sb0 = four.tile([P, size], BF16, tag="sb0")
-            nc.vector.tensor_scalar(out=sb0[:], in0=si0[:], scalar1=3.0, scalar2=None, op0=ALU.mult)
+            sb = deep.tile([P, 3, size], BF16, tag="sb")
+            nc.vector.tensor_scalar(out=sb[:, 0, :], in0=si0[:], scalar1=3.0, scalar2=None, op0=ALU.mult)
             z = two.tile([P, size], F32, tag="z")
             nc.vector.scalar_tensor_tensor(
-                out=z[:], in0=xg[:], scalar=1.0 / STEP, in1=sb0[:], op0=ALU.mult, op1=ALU.subtract
+                out=z[:], in0=xg[:], scalar=1.0 / STEP, in1=sb[:, 0, :], op0=ALU.mult, op1=ALU.subtract
             )
-            state[ch] = {"si": sis, "xg": xg, "sb0": sb0, "z": z, "size": size}
-
-        def stage_b(ch):
-            st = state[ch]
-            size = st["size"]
-            z = st["z"]
+            si = two.tile([P, 2, size], U32, tag="si")
+            for r in (1, 2):
+                if r > ACT_CASTS:
+                    nc.vector.tensor_scalar(
+                        out=si[:, r - 1, :].bitcast(I32), in0=xg[:], scalar1=1.0 / (3.0 * STEP), scalar2=SHIFT - r / 3.0,
+                        op0=ALU.mult, op1=ALU.add,
+                    )
+                else:
+                    nc.scalar.activation(
+                        out=si[:, r - 1, :], in_=xg[:], func=ACT.Identity, bias=SHIFT - r / 3.0, scale=1.0 / (3.0 * STEP)
+                    )
+            nc.scalar.activation(out=sb[:, 1:3, :], in_=si[:], func=ACT.Identity, bias=-3.0 * SHIFT, scale=3.0)
             dist = two.tile([P, size], F32, tag="dist")
             nc.scalar.activation(out=dist[:], in_=z[:], func=ACT.Abs)
-            fold = two.tile([P, size], F32, tag="fold")
-            nc.scalar.activation(out=fold[:], in_=dist[:], func=ACT.Abs, bias=-0.5, scale=1.0)
-            dip = two.tile([P, size], F32, tag="dip")
-            nc.scalar.activation(out=dip[:], in_=fold[:], func=ACT.Square, bias=-ROOT2 / 2.0, scale=ROOT2)
-            cap = three.tile([P, size], BF16, tag="cap")
-            nc.scalar.activation(out=cap[:], in_=dip[:], func=ACT.Identity, bias=1.5, scale=-1.0)
-            env0 = three.tile([P, size], BF16, tag="env0")
-            nc.scalar.activation(out=env0[:], in_=dist[:], func=ACT.Square, bias=1.5, scale=-1.0)
-            env1 = three.tile([P, size], BF16, tag="env1")
-            nc.scalar.activation(out=env1[:], in_=z[:], func=ACT.Square, bias=0.5, scale=1.0)
-            env2 = three.tile([P, size], BF16, tag="env2")
-            nc.scalar.activation(out=env2[:], in_=z[:], func=ACT.Square, bias=-0.5, scale=1.0)
-            sbs = [st["sb0"]]
-            for r in (1, 2):
-                if r <= ACT_CASTS:
-                    nc.scalar.activation(
-                        out=st["si"][r][:], in_=st["xg"][:], func=ACT.Identity, bias=SHIFT - r / 3.0, scale=1.0 / (3.0 * STEP)
-                    )
-                sb = four.tile([P, size], BF16, name="sb%d" % r, tag="sb%d" % r)
-                nc.scalar.copy(out=sb[:], in_=st["si"][r][:])
-                sbs.append(sb)
-            st["env"] = (env0, env1, env2)
-            st["cap"] = cap
-            st["sb"] = sbs
+            env = deep.tile([P, 3, size], BF16, tag="env")
+            nc.scalar.activation(out=env[:, 0, :], in_=dist[:], func=ACT.Square, bias=1.5, scale=-1.0)
+            nc.scalar.activation(out=env[:, 1, :], in_=z[:], func=ACT.Square, bias=0.5, scale=1.0)
+            nc.scalar.activation(out=env[:, 2, :], in_=z[:], func=ACT.Square, bias=-0.5, scale=1.0)
+            nc.scalar.activation(out=dist[:], in_=dist[:], func=ACT.Abs, bias=-0.5, scale=1.0)
+            nc.scalar.activation(out=dist[:], in_=dist[:], func=ACT.Square, bias=-ROOT2 / 2.0, scale=ROOT2)
+            cap = deep.tile([P, size], BF16, tag="cap")
+            nc.scalar.activation(out=cap[:], in_=dist[:], func=ACT.Identity, bias=1.5, scale=-1.0)
+            state[ch] = {"sb": sb, "env": env, "cap": cap, "size": size}
 
         def stage_x(ch):
             st = state[ch]
             size = st["size"]
             lanes = PASSES * CHUNKS[ch][0]
             plane = size // lanes
-            slab = slabs[ch % 2]
+            slab = slabs[ch % SLABS]
             planes = slab[:, 0:lanes, 0 : BASES * plane].rearrange("p a (k e) -> p k a e", k=BASES)
-            vals = []
-            for r in range(3):
-                val = two.tile([P, size], BF16, name="val%d" % r, tag="val%d" % r)
-                nc.vector.tensor_tensor(out=val[:], in0=st["env"][r][:], in1=st["cap"][:], op=ALU.min)
-                vals.append(val)
+            env = st["env"]
+            nc.vector.tensor_tensor(
+                out=env[:], in0=env[:], in1=st["cap"][:].unsqueeze(1).to_broadcast([P, 3, size]), op=ALU.min
+            )
+            mask = two.tile([P, BASES, size], BF16, tag="mask")
+            for m in range(0, BASES, 3):
+                classes = min(3, BASES - m)
+                nc.vector.tensor_scalar(
+                    out=mask[:, m : m + classes, :], in0=st["sb"][:, 0:classes, :], scalar1=float(m - 6), scalar2=0.5,
+                    op0=ALU.is_equal, op1=ALU.mult,
+                )
             for r in range(3):
                 slots = len(range(r, BASES, 3))
-                mask = three.tile([P, slots, size], BF16, tag="mask")
-                for m in range(slots):
-                    wanted = 3.0 * (m - 2) if r == 0 else m - 2 + SHIFT
-                    nc.vector.tensor_scalar(
-                        out=mask[:, m, :], in0=st["sb"][r][:], scalar1=wanted, scalar2=0.5, op0=ALU.is_equal, op1=ALU.mult
-                    )
                 nc.vector.tensor_tensor(
                     out=planes[:, r:BASES:3, :, :],
-                    in0=mask[:].rearrange("p m (a e) -> p m a e", a=lanes),
-                    in1=vals[r][:].rearrange("p (a e) -> p a e", a=lanes).unsqueeze(1).to_broadcast([P, slots, lanes, plane]),
+                    in0=mask[:, r:BASES:3, :].rearrange("p m (a e) -> p m a e", a=lanes),
+                    in1=env[:, r, :].rearrange("p (a e) -> p a e", a=lanes).unsqueeze(1).to_broadcast([P, slots, lanes, plane]),
                     op=ALU.mult,
                 )
 
         def stage_q(ch):
-            slab = slabs[ch % 2]
+            slab = slabs[ch % SLABS]
             groups = CHUNKS[ch][0]
-            codes = three.tile([P, PASSES, groups * N_MOVING], U32, tag="codes", align_bytes=64)
-            scales = three.tile([P, PASSES, groups * N_MOVING], U8, tag="scales", align_bytes=64)
-            for c in range(PASSES):
-                nc.vector.quantize_mx(
-                    out=codes[:, c, :].bitcast(E4X4),
-                    scales=scales[:, c, :],
-                    in_=slab[:, c * groups : (c + 1) * groups, :].rearrange("p a e -> p (a e)"),
-                )
+            codes = deep.tile([P, PASSES, groups * N_MOVING], U32, tag="codes", align_bytes=64)
+            scales = deep.tile([P, PASSES, groups * N_MOVING], U8, tag="scales", align_bytes=64)
+            together = min(groups, WIDEST // SLAB)
+            for g in range(0, groups, together):
+                for c in range(PASSES):
+                    cols = slice(g * N_MOVING, (g + together) * N_MOVING)
+                    nc.vector.quantize_mx(
+                        out=codes[:, c, cols].bitcast(E4X4),
+                        scales=scales[:, c, cols],
+                        in_=slab[:, c * groups + g : c * groups + g + together, :].rearrange("p a e -> p (a e)"),
+                    )
             state[ch]["codes"] = codes
             state[ch]["scales"] = scales
 
@@ -181,48 +166,50 @@ def tile_bsplinekanlayer_kernel(tc, x, spline_parameters, w_b, w_s, grad_out, ou
             codes = state[ch]["codes"]
             scales = state[ch]["scales"]
             width = ni * BASES
-            accs = {}
-            for c in range(PASSES):
+            together = min(groups, 2)
+            for g0 in range(0, groups, together):
+                accs = {}
+                for c in range(PASSES):
+                    for ot in range(OUTS // P):
+                        rows = slice(ot * P, (ot + 1) * P)
+                        for g in range(g0, g0 + together):
+                            cols = slice(g * N_MOVING, (g + 1) * N_MOVING)
+                            if c == 0:
+                                acc = psum.tile([P, N_MOVING], F32, tag="acc")
+                                accs[(ot, g)] = acc
+                            nc.tensor.matmul_mx(
+                                out=accs[(ot, g)][:],
+                                lhsT=g_codes[:, c, rows].bitcast(E5X4),
+                                lhsT_scale=g_scales[:, c, rows],
+                                rhs=codes[:, c, cols].bitcast(E4X4),
+                                rhs_scale=scales[:, c, cols],
+                                start=(c == 0),
+                                stop=(c == PASSES - 1),
+                            )
                 for ot in range(OUTS // P):
                     rows = slice(ot * P, (ot + 1) * P)
-                    for g in range(groups):
-                        cols = slice(g * N_MOVING, (g + 1) * N_MOVING)
-                        if c == 0:
-                            acc = psum.tile([P, N_MOVING], F32, tag="acc")
-                            accs[(ot, g)] = acc
-                        nc.tensor.matmul_mx(
-                            out=accs[(ot, g)][:],
-                            lhsT=g_codes[:, c, rows].bitcast(E5X4),
-                            lhsT_scale=g_scales[:, c, rows],
-                            rhs=codes[:, c, cols].bitcast(E4X4),
-                            rhs_scale=scales[:, c, cols],
-                            start=(c == 0),
-                            stop=(c == PASSES - 1),
+                    stage = outp.tile([P, together * width], F32, tag="stage")
+                    for g in range(together):
+                        nc.scalar.activation(
+                            out=stage[:, g * width : (g + 1) * width].rearrange("p (i k) -> p i k", k=BASES),
+                            in_=accs[(ot, g0 + g)][:, 0:width].rearrange("p (k i) -> p i k", k=BASES),
+                            func=ACT.Copy,
+                            scale=ws[:, 0:1],
                         )
-            for ot in range(OUTS // P):
-                rows = slice(ot * P, (ot + 1) * P)
-                stage = outp.tile([P, groups * width], F32, tag="stage")
-                for g in range(groups):
-                    acc = accs[(ot, g)]
-                    nc.scalar.activation(
-                        out=stage[:, g * width : (g + 1) * width].rearrange("p (i k) -> p i k", k=BASES),
-                        in_=acc[:, 0:width].rearrange("p (k i) -> p i k", k=BASES),
-                        func=ACT.Copy,
-                        scale=ws[:, 0:1],
+                    lo = starts[ch] + g0 * ni
+                    nc.sync.dma_start(
+                        out=out[rows, lo : lo + together * ni, :].rearrange("o i k -> o (i k)"), in_=stage[:]
                     )
-                nc.sync.dma_start(
-                    out=out[rows, starts[ch] : starts[ch] + spans[ch], :].rearrange("o i k -> o (i k)"),
-                    in_=stage[:],
-                )
 
         n_chunks = len(CHUNKS)
         stage_a(0)
-        stage_b(0)
         for c in range(PASSES):
-            nc.scalar.copy(out=g_grouped[:, c], in_=g_raw[:, c].rearrange("p j o -> p o j"))
+            nc.scalar.copy(
+                out=g_grouped[:, c].rearrange("p (n i) j -> p n j i", i=PACK),
+                in_=g_raw[:, c].rearrange("p j (n i) -> p n j i", i=PACK),
+            )
         for ch in range(1, AHEAD):
             stage_a(ch)
-            stage_b(ch)
         for c in range(PASSES):
             nc.vector.quantize_mx(
                 out=g_codes[:, c, :].bitcast(E5X4),
@@ -233,6 +220,5 @@ def tile_bsplinekanlayer_kernel(tc, x, spline_parameters, w_b, w_s, grad_out, ou
             stage_x(ch)
             if ch + AHEAD < n_chunks:
                 stage_a(ch + AHEAD)
-                stage_b(ch + AHEAD)
             stage_q(ch)
             stage_out(ch)

@@ -22,7 +22,8 @@ CHUNKS = [(2, 38), (2, 38), (2, 38), (2, 38), (2, 38), (2, 28), (1, 38), (1, 38)
 MAX_GROUPS = max(groups for groups, ni in CHUNKS)
 SLAB = N_MOVING * PACK
 WIDEST = 4096
-ACT_CASTS = 1
+ACT_CASTS = 3
+HEAD_ON_VECTOR = 1
 X_SPLIT = 160
 SLABS = 2
 AHEAD = 2
@@ -51,11 +52,12 @@ def tile_bsplinekanlayer_kernel(tc, x, spline_parameters, w_b, w_s, grad_out, ou
 
         x_raw = keep.tile([P, PASSES, PACK, FEATURES], BF16)
         x_view = x.rearrange("(c p j) i -> p c j i", c=PASSES, p=P, j=PACK)
-        for piece in (slice(0, X_SPLIT), slice(X_SPLIT, FEATURES)):
-            for c in range(PASSES):
-                nc.sync.dma_start(out=x_raw[:, c, :, piece], in_=x_view[:, c, :, piece])
         g_raw = keep.tile([P, PASSES, PACK, OUTS], BF16)
+        for c in range(PASSES):
+            nc.sync.dma_start(out=x_raw[:, c, :, 0:X_SPLIT], in_=x_view[:, c, :, 0:X_SPLIT])
         nc.sync.dma_start(out=g_raw[:], in_=grad_out.rearrange("(c p j) o -> p c j o", c=PASSES, p=P, j=PACK))
+        for c in range(PASSES):
+            nc.sync.dma_start(out=x_raw[:, c, :, X_SPLIT:FEATURES], in_=x_view[:, c, :, X_SPLIT:FEATURES])
         ws_bf = keep.tile([P, 1], BF16)
         nc.sync.dma_start(out=ws_bf[:], in_=w_s.partition_broadcast(P))
 
@@ -85,26 +87,32 @@ def tile_bsplinekanlayer_kernel(tc, x, spline_parameters, w_b, w_s, grad_out, ou
                 op0=ALU.max,
                 op1=ALU.min,
             )
-            si0 = two.tile([P, size], I32, tag="si0")
-            nc.vector.tensor_scalar(out=si0[:], in0=xg[:], scalar1=1.0 / (3.0 * STEP), scalar2=None, op0=ALU.mult)
-            sb = deep.tile([P, 3, size], BF16, tag="sb")
-            nc.vector.tensor_scalar(out=sb[:, 0, :], in0=si0[:], scalar1=3.0, scalar2=None, op0=ALU.mult)
-            z = two.tile([P, size], F32, tag="z")
-            nc.vector.scalar_tensor_tensor(
-                out=z[:], in0=xg[:], scalar=1.0 / STEP, in1=sb[:, 0, :], op0=ALU.mult, op1=ALU.subtract
-            )
-            si = two.tile([P, 2, size], U32, tag="si")
-            for r in (1, 2):
-                if r > ACT_CASTS:
+            on_vector = ch < HEAD_ON_VECTOR
+            si = two.tile([P, 3, size], U32, tag="si")
+            for r in range(3):
+                if on_vector or r >= ACT_CASTS:
                     nc.vector.tensor_scalar(
-                        out=si[:, r - 1, :].bitcast(I32), in0=xg[:], scalar1=1.0 / (3.0 * STEP), scalar2=SHIFT - r / 3.0,
+                        out=si[:, r, :].bitcast(I32), in0=xg[:], scalar1=1.0 / (3.0 * STEP), scalar2=SHIFT - r / 3.0,
                         op0=ALU.mult, op1=ALU.add,
                     )
                 else:
                     nc.scalar.activation(
-                        out=si[:, r - 1, :], in_=xg[:], func=ACT.Identity, bias=SHIFT - r / 3.0, scale=1.0 / (3.0 * STEP)
+                        out=si[:, r, :], in_=xg[:], func=ACT.Identity, bias=SHIFT - r / 3.0, scale=1.0 / (3.0 * STEP)
                     )
-            nc.scalar.activation(out=sb[:, 1:3, :], in_=si[:], func=ACT.Identity, bias=-3.0 * SHIFT, scale=3.0)
+            sb = deep.tile([P, 3, size], BF16, tag="sb")
+            mine = 3 if on_vector else 1
+            nc.vector.tensor_scalar(
+                out=sb[:, 0:mine, :], in0=si[:, 0:mine, :].bitcast(I32), scalar1=3.0, scalar2=-3.0 * SHIFT,
+                op0=ALU.mult, op1=ALU.add,
+            )
+            if not on_vector:
+                nc.scalar.activation(
+                    out=sb[:, 1:3, :], in_=si[:, 1:3, :], func=ACT.Identity, bias=-3.0 * SHIFT, scale=3.0
+                )
+            z = two.tile([P, size], F32, tag="z")
+            nc.vector.scalar_tensor_tensor(
+                out=z[:], in0=xg[:], scalar=1.0 / STEP, in1=sb[:, 0, :], op0=ALU.mult, op1=ALU.subtract
+            )
             dist = two.tile([P, size], F32, tag="dist")
             nc.scalar.activation(out=dist[:], in_=z[:], func=ACT.Abs)
             env = deep.tile([P, 3, size], BF16, tag="env")
@@ -114,7 +122,10 @@ def tile_bsplinekanlayer_kernel(tc, x, spline_parameters, w_b, w_s, grad_out, ou
             nc.scalar.activation(out=dist[:], in_=dist[:], func=ACT.Abs, bias=-0.5, scale=1.0)
             nc.scalar.activation(out=dist[:], in_=dist[:], func=ACT.Square, bias=-ROOT2 / 2.0, scale=ROOT2)
             cap = deep.tile([P, size], BF16, tag="cap")
-            nc.scalar.activation(out=cap[:], in_=dist[:], func=ACT.Identity, bias=1.5, scale=-1.0)
+            if ch < HEAD_ON_VECTOR:
+                nc.vector.tensor_scalar(out=cap[:], in0=dist[:], scalar1=-1.0, scalar2=1.5, op0=ALU.mult, op1=ALU.add)
+            else:
+                nc.scalar.activation(out=cap[:], in_=dist[:], func=ACT.Identity, bias=1.5, scale=-1.0)
             state[ch] = {"sb": sb, "env": env, "cap": cap, "size": size}
 
         def stage_x(ch):
@@ -204,7 +215,7 @@ def tile_bsplinekanlayer_kernel(tc, x, spline_parameters, w_b, w_s, grad_out, ou
         n_chunks = len(CHUNKS)
         stage_a(0)
         for c in range(PASSES):
-            nc.scalar.copy(
+            nc.vector.tensor_copy(
                 out=g_grouped[:, c].rearrange("p (n i) j -> p n j i", i=PACK),
                 in_=g_raw[:, c].rearrange("p j (n i) -> p n j i", i=PACK),
             )

@@ -2,6 +2,7 @@ import math
 from contextlib import ExitStack
 
 import concourse.mybir as mybir
+from concourse.masks import make_identity
 
 BF16 = mybir.dt.bfloat16
 F32 = mybir.dt.float32
@@ -48,7 +49,8 @@ def tile_bsplinekanlayer_kernel(tc, x, spline_parameters, w_b, w_s, grad_out, ou
         two = ctx.enter_context(tc.tile_pool(name="two", bufs=2))
         deep = ctx.enter_context(tc.tile_pool(name="deep", bufs=DEEP))
         outp = ctx.enter_context(tc.tile_pool(name="outp", bufs=6))
-        psum = ctx.enter_context(tc.psum_pool(name="psum", bufs=8))
+        psum = ctx.enter_context(tc.psum_pool(name="psum", bufs=6))
+        zpsum = ctx.enter_context(tc.psum_pool(name="zpsum", bufs=1))
 
         x_raw = keep.tile([P, PASSES, PACK, FEATURES], BF16)
         x_view = x.rearrange("(c p j) i -> p c j i", c=PASSES, p=P, j=PACK)
@@ -60,6 +62,13 @@ def tile_bsplinekanlayer_kernel(tc, x, spline_parameters, w_b, w_s, grad_out, ou
             nc.sync.dma_start(out=x_raw[:, c, :, X_SPLIT:FEATURES], in_=x_view[:, c, :, X_SPLIT:FEATURES])
         ws_bf = keep.tile([P, 1], BF16)
         nc.sync.dma_start(out=ws_bf[:], in_=w_s.partition_broadcast(P))
+
+        ident = keep.tile([P, P], F32)
+        make_identity(nc, ident[:])
+        per_step = keep.tile([P, P], F32)
+        nc.gpsimd.tensor_scalar(out=per_step[:], in0=ident[:], scalar1=1.0 / STEP, scalar2=0.0, op0=ALU.mult, op1=ALU.add)
+        minus1 = keep.tile([P, P], BF16)
+        nc.gpsimd.tensor_scalar(out=minus1[:], in0=ident[:], scalar1=-1.0, scalar2=0.0, op0=ALU.mult, op1=ALU.add)
 
         slabs = []
         for n in range(SLABS):
@@ -78,7 +87,7 @@ def tile_bsplinekanlayer_kernel(tc, x, spline_parameters, w_b, w_s, grad_out, ou
         def stage_a(ch):
             groups, ni = CHUNKS[ch]
             size = PASSES * groups * ni * PACK
-            xg = two.tile([P, size], BF16, tag="xg")
+            xg = two.tile([P, size], F32, tag="xg")
             nc.vector.tensor_scalar(
                 out=xg[:].rearrange("p (c i j) -> p c i j", c=PASSES, j=PACK),
                 in0=x_raw[:, :, :, starts[ch] : starts[ch] + spans[ch]].rearrange("p c j i -> p c i j"),
@@ -109,16 +118,18 @@ def tile_bsplinekanlayer_kernel(tc, x, spline_parameters, w_b, w_s, grad_out, ou
                 nc.scalar.activation(
                     out=sb[:, 1:3, :], in_=si[:, 1:3, :], func=ACT.Identity, bias=-3.0 * SHIFT, scale=3.0
                 )
-            z = two.tile([P, size], F32, tag="z")
-            nc.vector.scalar_tensor_tensor(
-                out=z[:], in0=xg[:], scalar=1.0 / STEP, in1=sb[:, 0, :], op0=ALU.mult, op1=ALU.subtract
-            )
+            half = size // PASSES
             dist = two.tile([P, size], F32, tag="dist")
-            nc.scalar.activation(out=dist[:], in_=z[:], func=ACT.Abs)
             env = deep.tile([P, 3, size], BF16, tag="env")
+            for c in range(PASSES):
+                part = slice(c * half, (c + 1) * half)
+                z3 = zpsum.tile([P, N_MOVING], F32, tag="z%d" % c)
+                nc.tensor.matmul(out=z3[:, 0:half], lhsT=per_step[:], rhs=xg[:, part], start=True, stop=False)
+                nc.tensor.matmul(out=z3[:, 0:half], lhsT=minus1[:], rhs=sb[:, 0, part], start=False, stop=True)
+                nc.scalar.activation(out=dist[:, part], in_=z3[:, 0:half], func=ACT.Abs)
+                nc.scalar.activation(out=env[:, 1, part], in_=z3[:, 0:half], func=ACT.Square, bias=0.5, scale=1.0)
+                nc.scalar.activation(out=env[:, 2, part], in_=z3[:, 0:half], func=ACT.Square, bias=-0.5, scale=1.0)
             nc.scalar.activation(out=env[:, 0, :], in_=dist[:], func=ACT.Square, bias=1.5, scale=-1.0)
-            nc.scalar.activation(out=env[:, 1, :], in_=z[:], func=ACT.Square, bias=0.5, scale=1.0)
-            nc.scalar.activation(out=env[:, 2, :], in_=z[:], func=ACT.Square, bias=-0.5, scale=1.0)
             nc.scalar.activation(out=dist[:], in_=dist[:], func=ACT.Abs, bias=-0.5, scale=1.0)
             nc.scalar.activation(out=dist[:], in_=dist[:], func=ACT.Square, bias=-ROOT2 / 2.0, scale=ROOT2)
             cap = deep.tile([P, size], BF16, tag="cap")
@@ -180,9 +191,9 @@ def tile_bsplinekanlayer_kernel(tc, x, spline_parameters, w_b, w_s, grad_out, ou
             together = min(groups, 2)
             for g0 in range(0, groups, together):
                 accs = {}
-                for c in range(PASSES):
-                    for ot in range(OUTS // P):
-                        rows = slice(ot * P, (ot + 1) * P)
+                for ot in range(OUTS // P):
+                    rows = slice(ot * P, (ot + 1) * P)
+                    for c in range(PASSES):
                         for g in range(g0, g0 + together):
                             cols = slice(g * N_MOVING, (g + 1) * N_MOVING)
                             if c == 0:
@@ -197,8 +208,6 @@ def tile_bsplinekanlayer_kernel(tc, x, spline_parameters, w_b, w_s, grad_out, ou
                                 start=(c == 0),
                                 stop=(c == PASSES - 1),
                             )
-                for ot in range(OUTS // P):
-                    rows = slice(ot * P, (ot + 1) * P)
                     stage = outp.tile([P, together * width], F32, tag="stage")
                     for g in range(together):
                         nc.scalar.activation(

@@ -19,7 +19,7 @@ PACK = 4
 TOKENS, FEATURES, OUTS, BASES = 1024, 512, 512, 13
 PASSES = TOKENS // (P * PACK)
 N_MOVING = 512
-CHUNKS = [(2, 38), (2, 38), (2, 38), (2, 38), (2, 38), (2, 28), (1, 38), (1, 38)]
+CHUNKS = [(1, 38), (2, 38), (2, 38), (2, 38), (2, 38), (2, 38), (2, 38), (1, 18)]
 MAX_GROUPS = max(groups for groups, ni in CHUNKS)
 SLAB = N_MOVING * PACK
 WIDEST = 4096
@@ -29,6 +29,7 @@ X_SPLIT = 160
 SLABS = 2
 AHEAD = 2
 DEEP = AHEAD + 1
+W_CHUNKS = 5
 
 FLOPS = 2 * TOKENS * OUTS * FEATURES * BASES
 BYTES = 2 * TOKENS * FEATURES * 2 + 2 + OUTS * FEATURES * BASES * 4
@@ -49,7 +50,7 @@ def tile_bsplinekanlayer_kernel(tc, x, spline_parameters, w_b, w_s, grad_out, ou
         two = ctx.enter_context(tc.tile_pool(name="two", bufs=2))
         deep = ctx.enter_context(tc.tile_pool(name="deep", bufs=DEEP))
         outp = ctx.enter_context(tc.tile_pool(name="outp", bufs=6))
-        psum = ctx.enter_context(tc.psum_pool(name="psum", bufs=6))
+        psum = ctx.enter_context(tc.psum_pool(name="psum", bufs=4))
         zpsum = ctx.enter_context(tc.psum_pool(name="zpsum", bufs=1))
 
         x_raw = keep.tile([P, PASSES, PACK, FEATURES], BF16)
@@ -69,6 +70,8 @@ def tile_bsplinekanlayer_kernel(tc, x, spline_parameters, w_b, w_s, grad_out, ou
         nc.gpsimd.tensor_scalar(out=per_step[:], in0=ident[:], scalar1=1.0 / STEP, scalar2=0.0, op0=ALU.mult, op1=ALU.add)
         minus1 = keep.tile([P, P], BF16)
         nc.gpsimd.tensor_scalar(out=minus1[:], in0=ident[:], scalar1=-1.0, scalar2=0.0, op0=ALU.mult, op1=ALU.add)
+        minus3 = keep.tile([P, P], BF16)
+        nc.gpsimd.tensor_scalar(out=minus3[:], in0=ident[:], scalar1=-3.0, scalar2=0.0, op0=ALU.mult, op1=ALU.add)
 
         slabs = []
         for n in range(SLABS):
@@ -111,27 +114,39 @@ def tile_bsplinekanlayer_kernel(tc, x, spline_parameters, w_b, w_s, grad_out, ou
             sb = deep.tile([P, 3, size], BF16, tag="sb")
             mine = 3 if on_vector else 1
             nc.vector.tensor_scalar(
-                out=sb[:, 0:mine, :], in0=si[:, 0:mine, :].bitcast(I32), scalar1=3.0, scalar2=-3.0 * SHIFT,
+                out=sb[:, 0:mine, :], in0=si[:, 0:mine, :].bitcast(I32), scalar1=1.0, scalar2=-SHIFT,
                 op0=ALU.mult, op1=ALU.add,
             )
             if not on_vector:
                 nc.scalar.activation(
-                    out=sb[:, 1:3, :], in_=si[:, 1:3, :], func=ACT.Identity, bias=-3.0 * SHIFT, scale=3.0
+                    out=sb[:, 1:3, :], in_=si[:, 1:3, :], func=ACT.Identity, bias=-SHIFT, scale=1.0
                 )
             half = size // PASSES
             dist = two.tile([P, size], F32, tag="dist")
             env = deep.tile([P, 3, size], BF16, tag="env")
+            banks = []
             for c in range(PASSES):
                 part = slice(c * half, (c + 1) * half)
                 z3 = zpsum.tile([P, N_MOVING], F32, tag="z%d" % c)
                 nc.tensor.matmul(out=z3[:, 0:half], lhsT=per_step[:], rhs=xg[:, part], start=True, stop=False)
-                nc.tensor.matmul(out=z3[:, 0:half], lhsT=minus1[:], rhs=sb[:, 0, part], start=False, stop=True)
+                nc.tensor.matmul(out=z3[:, 0:half], lhsT=minus3[:], rhs=sb[:, 0, part], start=False, stop=True)
                 nc.scalar.activation(out=dist[:, part], in_=z3[:, 0:half], func=ACT.Abs)
                 nc.scalar.activation(out=env[:, 1, part], in_=z3[:, 0:half], func=ACT.Square, bias=0.5, scale=1.0)
                 nc.scalar.activation(out=env[:, 2, part], in_=z3[:, 0:half], func=ACT.Square, bias=-0.5, scale=1.0)
+                if 1 <= ch <= W_CHUNKS:
+                    w1 = zpsum.tile([P, N_MOVING], F32, tag="w%d" % c)
+                    banks.append(w1)
+                    nc.tensor.matmul(out=w1[:, 0:half], lhsT=per_step[:], rhs=xg[:, part], start=True, stop=False)
+                    for r in range(3):
+                        nc.tensor.matmul(out=w1[:, 0:half], lhsT=minus1[:], rhs=sb[:, r, part], start=False, stop=(r == 2))
             nc.scalar.activation(out=env[:, 0, :], in_=dist[:], func=ACT.Square, bias=1.5, scale=-1.0)
-            nc.scalar.activation(out=dist[:], in_=dist[:], func=ACT.Abs, bias=-0.5, scale=1.0)
-            nc.scalar.activation(out=dist[:], in_=dist[:], func=ACT.Square, bias=-ROOT2 / 2.0, scale=ROOT2)
+            if 1 <= ch <= W_CHUNKS:
+                for c in range(PASSES):
+                    part = slice(c * half, (c + 1) * half)
+                    nc.scalar.activation(out=dist[:, part], in_=banks[c][:, 0:half], func=ACT.Square, bias=-ROOT2, scale=ROOT2)
+            else:
+                nc.scalar.activation(out=dist[:], in_=dist[:], func=ACT.Abs, bias=-0.5, scale=1.0)
+                nc.scalar.activation(out=dist[:], in_=dist[:], func=ACT.Square, bias=-ROOT2 / 2.0, scale=ROOT2)
             cap = deep.tile([P, size], BF16, tag="cap")
             if ch < HEAD_ON_VECTOR:
                 nc.vector.tensor_scalar(out=cap[:], in0=dist[:], scalar1=-1.0, scalar2=1.5, op0=ALU.mult, op1=ALU.add)
@@ -154,7 +169,7 @@ def tile_bsplinekanlayer_kernel(tc, x, spline_parameters, w_b, w_s, grad_out, ou
             for m in range(0, BASES, 3):
                 classes = min(3, BASES - m)
                 nc.vector.tensor_scalar(
-                    out=mask[:, m : m + classes, :], in0=st["sb"][:, 0:classes, :], scalar1=float(m - 6), scalar2=0.5,
+                    out=mask[:, m : m + classes, :], in0=st["sb"][:, 0:classes, :], scalar1=float(m // 3 - 2), scalar2=0.5,
                     op0=ALU.is_equal, op1=ALU.mult,
                 )
             for r in range(3):

@@ -49,7 +49,7 @@ def tile_bsplinekanlayer_kernel(tc, x, spline_parameters, w_b, w_s, grad_out, ou
         one = ctx.enter_context(tc.tile_pool(name="one", bufs=1))
         two = ctx.enter_context(tc.tile_pool(name="two", bufs=2))
         deep = ctx.enter_context(tc.tile_pool(name="deep", bufs=DEEP))
-        outp = ctx.enter_context(tc.tile_pool(name="outp", bufs=6))
+        outp = ctx.enter_context(tc.tile_pool(name="outp", bufs=8))
         psum = ctx.enter_context(tc.psum_pool(name="psum", bufs=4))
         zpsum = ctx.enter_context(tc.psum_pool(name="zpsum", bufs=1))
 
@@ -181,60 +181,48 @@ def tile_bsplinekanlayer_kernel(tc, x, spline_parameters, w_b, w_s, grad_out, ou
                     op=ALU.mult,
                 )
 
-        def stage_q(ch):
+        def stage_q(ch, g):
             slab = slabs[ch % SLABS]
             groups = CHUNKS[ch][0]
-            codes = deep.tile([P, PASSES, groups * N_MOVING], U32, tag="codes", align_bytes=64)
-            scales = deep.tile([P, PASSES, groups * N_MOVING], U8, tag="scales", align_bytes=64)
-            together = min(groups, WIDEST // SLAB)
-            for g in range(0, groups, together):
-                for c in range(PASSES):
-                    cols = slice(g * N_MOVING, (g + together) * N_MOVING)
-                    nc.vector.quantize_mx(
-                        out=codes[:, c, cols].bitcast(E4X4),
-                        scales=scales[:, c, cols],
-                        in_=slab[:, c * groups + g : c * groups + g + together, :].rearrange("p a e -> p (a e)"),
-                    )
-            state[ch]["codes"] = codes
-            state[ch]["scales"] = scales
+            if g == 0:
+                codes = deep.tile([P, PASSES, groups * N_MOVING], U32, tag="codes", align_bytes=64)
+                scales = deep.tile([P, PASSES, groups * N_MOVING], U8, tag="scales", align_bytes=64)
+                state[ch]["codes"] = codes
+                state[ch]["scales"] = scales
+            cols = slice(g * N_MOVING, (g + 1) * N_MOVING)
+            for c in range(PASSES):
+                nc.vector.quantize_mx(
+                    out=state[ch]["codes"][:, c, cols].bitcast(E4X4),
+                    scales=state[ch]["scales"][:, c, cols],
+                    in_=slab[:, c * groups + g, :],
+                )
 
-        def stage_out(ch):
-            groups, ni = CHUNKS[ch]
-            codes = state[ch]["codes"]
-            scales = state[ch]["scales"]
+        def stage_out(ch, g):
+            ni = CHUNKS[ch][1]
             width = ni * BASES
-            together = min(groups, 2)
-            for g0 in range(0, groups, together):
-                accs = {}
-                for ot in range(OUTS // P):
-                    rows = slice(ot * P, (ot + 1) * P)
-                    for c in range(PASSES):
-                        for g in range(g0, g0 + together):
-                            cols = slice(g * N_MOVING, (g + 1) * N_MOVING)
-                            if c == 0:
-                                acc = psum.tile([P, N_MOVING], F32, tag="acc")
-                                accs[(ot, g)] = acc
-                            nc.tensor.matmul_mx(
-                                out=accs[(ot, g)][:],
-                                lhsT=g_codes[:, c, rows].bitcast(E5X4),
-                                lhsT_scale=g_scales[:, c, rows],
-                                rhs=codes[:, c, cols].bitcast(E4X4),
-                                rhs_scale=scales[:, c, cols],
-                                start=(c == 0),
-                                stop=(c == PASSES - 1),
-                            )
-                    stage = outp.tile([P, together * width], F32, tag="stage")
-                    for g in range(together):
-                        nc.scalar.activation(
-                            out=stage[:, g * width : (g + 1) * width].rearrange("p (i k) -> p i k", k=BASES),
-                            in_=accs[(ot, g0 + g)][:, 0:width].rearrange("p (k i) -> p i k", k=BASES),
-                            func=ACT.Copy,
-                            scale=ws[:, 0:1],
-                        )
-                    lo = starts[ch] + g0 * ni
-                    nc.sync.dma_start(
-                        out=out[rows, lo : lo + together * ni, :].rearrange("o i k -> o (i k)"), in_=stage[:]
+            cols = slice(g * N_MOVING, (g + 1) * N_MOVING)
+            lo = starts[ch] + g * ni
+            for ot in range(OUTS // P):
+                rows = slice(ot * P, (ot + 1) * P)
+                acc = psum.tile([P, N_MOVING], F32, tag="acc")
+                for c in range(PASSES):
+                    nc.tensor.matmul_mx(
+                        out=acc[:],
+                        lhsT=g_codes[:, c, rows].bitcast(E5X4),
+                        lhsT_scale=g_scales[:, c, rows],
+                        rhs=state[ch]["codes"][:, c, cols].bitcast(E4X4),
+                        rhs_scale=state[ch]["scales"][:, c, cols],
+                        start=(c == 0),
+                        stop=(c == PASSES - 1),
                     )
+                stage = outp.tile([P, width], F32, tag="stage")
+                nc.scalar.activation(
+                    out=stage[:].rearrange("p (i k) -> p i k", k=BASES),
+                    in_=acc[:, 0:width].rearrange("p (k i) -> p i k", k=BASES),
+                    func=ACT.Copy,
+                    scale=ws[:, 0:1],
+                )
+                nc.sync.dma_start(out=out[rows, lo : lo + ni, :].rearrange("o i k -> o (i k)"), in_=stage[:])
 
         n_chunks = len(CHUNKS)
         stage_a(0)
@@ -255,5 +243,6 @@ def tile_bsplinekanlayer_kernel(tc, x, spline_parameters, w_b, w_s, grad_out, ou
             stage_x(ch)
             if ch + AHEAD < n_chunks:
                 stage_a(ch + AHEAD)
-            stage_q(ch)
-            stage_out(ch)
+            for g in range(CHUNKS[ch][0]):
+                stage_q(ch, g)
+                stage_out(ch, g)

import math
from contextlib import ExitStack

import concourse.mybir as mybir
from concourse.masks import make_identity

BF16 = mybir.dt.bfloat16
F32 = mybir.dt.float32
I32 = mybir.dt.int32
U32 = mybir.dt.uint32
U8 = mybir.dt.uint8
E4X4 = mybir.dt.float8_e4m3fn_x4
E5X4 = mybir.dt.float8_e5m2_x4
ALU = mybir.AluOpType
ACT = mybir.ActivationFunctionType

P = 128
PACK = 4
TOKENS, FEATURES, OUTS, BASES = 1024, 512, 512, 13
PASSES = TOKENS // (P * PACK)
N_MOVING = 512
CHUNKS = [(1, 38), (2, 38), (2, 38), (2, 38), (2, 38), (2, 38), (2, 38), (1, 18)]
MAX_GROUPS = max(groups for groups, ni in CHUNKS)
SLAB = N_MOVING * PACK
WIDEST = 4096
ACT_CASTS = 3
HEAD_ON_VECTOR = 1
X_SPLIT = 160
SLABS = 2
AHEAD = 2
DEEP = AHEAD + 1
W_CHUNKS = 5

FLOPS = 2 * TOKENS * OUTS * FEATURES * BASES
BYTES = 2 * TOKENS * FEATURES * 2 + 2 + OUTS * FEATURES * BASES * 4

STEP = 0.15
ROOT2 = math.sqrt(2.0)
SHIFT = 8.0


def tile_bsplinekanlayer_kernel(tc, x, spline_parameters, w_b, w_s, grad_out, out):
    nc = tc.nc
    spans = [groups * ni for groups, ni in CHUNKS]
    starts = [sum(spans[:n]) for n in range(len(CHUNKS))]
    assert sum(spans) == FEATURES
    with ExitStack() as ctx:
        keep = ctx.enter_context(tc.tile_pool(name="keep", bufs=1))
        one = ctx.enter_context(tc.tile_pool(name="one", bufs=1))
        two = ctx.enter_context(tc.tile_pool(name="two", bufs=2))
        deep = ctx.enter_context(tc.tile_pool(name="deep", bufs=DEEP))
        outp = ctx.enter_context(tc.tile_pool(name="outp", bufs=8))
        psum = ctx.enter_context(tc.psum_pool(name="psum", bufs=4))
        zpsum = ctx.enter_context(tc.psum_pool(name="zpsum", bufs=1))

        x_raw = keep.tile([P, PASSES, PACK, FEATURES], BF16)
        x_view = x.rearrange("(c p j) i -> p c j i", c=PASSES, p=P, j=PACK)
        g_raw = keep.tile([P, PASSES, PACK, OUTS], BF16)
        for c in range(PASSES):
            nc.sync.dma_start(out=x_raw[:, c, :, 0:X_SPLIT], in_=x_view[:, c, :, 0:X_SPLIT])
        nc.sync.dma_start(out=g_raw[:], in_=grad_out.rearrange("(c p j) o -> p c j o", c=PASSES, p=P, j=PACK))
        for c in range(PASSES):
            nc.sync.dma_start(out=x_raw[:, c, :, X_SPLIT:FEATURES], in_=x_view[:, c, :, X_SPLIT:FEATURES])
        ws_bf = keep.tile([P, 1], BF16)
        nc.sync.dma_start(out=ws_bf[:], in_=w_s.partition_broadcast(P))

        ident = keep.tile([P, P], F32)
        make_identity(nc, ident[:])
        per_step = keep.tile([P, P], F32)
        nc.gpsimd.tensor_scalar(out=per_step[:], in0=ident[:], scalar1=1.0 / STEP, scalar2=0.0, op0=ALU.mult, op1=ALU.add)
        minus1 = keep.tile([P, P], BF16)
        nc.gpsimd.tensor_scalar(out=minus1[:], in0=ident[:], scalar1=-1.0, scalar2=0.0, op0=ALU.mult, op1=ALU.add)
        minus3 = keep.tile([P, P], BF16)
        nc.gpsimd.tensor_scalar(out=minus3[:], in0=ident[:], scalar1=-3.0, scalar2=0.0, op0=ALU.mult, op1=ALU.add)

        slabs = []
        for n in range(SLABS):
            slab = keep.tile([P, PASSES * MAX_GROUPS, SLAB], BF16, name="slab%d" % n, align_bytes=64)
            nc.vector.memset(slab[:, :, BASES * PACK * max(ni for groups, ni in CHUNKS) : SLAB], 0.0)
            slabs.append(slab)
        ws = keep.tile([P, 1], F32)
        nc.vector.tensor_copy(out=ws[:], in_=ws_bf[:])

        g_grouped = keep.tile([P, PASSES, OUTS, PACK], BF16, align_bytes=64)
        g_codes = keep.tile([P, PASSES, OUTS], U32, align_bytes=64)
        g_scales = keep.tile([P, PASSES, OUTS], U8, align_bytes=64)

        state = {}

        def stage_a(ch):
            groups, ni = CHUNKS[ch]
            size = PASSES * groups * ni * PACK
            xg = two.tile([P, size], F32, tag="xg")
            nc.vector.tensor_scalar(
                out=xg[:].rearrange("p (c i j) -> p c i j", c=PASSES, j=PACK),
                in0=x_raw[:, :, :, starts[ch] : starts[ch] + spans[ch]].rearrange("p c j i -> p c i j"),
                scalar1=-2.0,
                scalar2=2.0,
                op0=ALU.max,
                op1=ALU.min,
            )
            on_vector = ch < HEAD_ON_VECTOR
            si = two.tile([P, 3, size], U32, tag="si")
            for r in range(3):
                if on_vector or r >= ACT_CASTS:
                    nc.vector.tensor_scalar(
                        out=si[:, r, :].bitcast(I32), in0=xg[:], scalar1=1.0 / (3.0 * STEP), scalar2=SHIFT - r / 3.0,
                        op0=ALU.mult, op1=ALU.add,
                    )
                else:
                    nc.scalar.activation(
                        out=si[:, r, :], in_=xg[:], func=ACT.Identity, bias=SHIFT - r / 3.0, scale=1.0 / (3.0 * STEP)
                    )
            sb = deep.tile([P, 3, size], BF16, tag="sb")
            mine = 3 if on_vector else 1
            nc.vector.tensor_scalar(
                out=sb[:, 0:mine, :], in0=si[:, 0:mine, :].bitcast(I32), scalar1=1.0, scalar2=-SHIFT,
                op0=ALU.mult, op1=ALU.add,
            )
            if not on_vector:
                nc.scalar.activation(
                    out=sb[:, 1:3, :], in_=si[:, 1:3, :], func=ACT.Identity, bias=-SHIFT, scale=1.0
                )
            half = size // PASSES
            dist = two.tile([P, size], F32, tag="dist")
            env = deep.tile([P, 3, size], BF16, tag="env")
            banks = []
            for c in range(PASSES):
                part = slice(c * half, (c + 1) * half)
                z3 = zpsum.tile([P, N_MOVING], F32, tag="z%d" % c)
                nc.tensor.matmul(out=z3[:, 0:half], lhsT=per_step[:], rhs=xg[:, part], start=True, stop=False)
                nc.tensor.matmul(out=z3[:, 0:half], lhsT=minus3[:], rhs=sb[:, 0, part], start=False, stop=True)
                nc.scalar.activation(out=dist[:, part], in_=z3[:, 0:half], func=ACT.Abs)
                nc.scalar.activation(out=env[:, 1, part], in_=z3[:, 0:half], func=ACT.Square, bias=0.5, scale=1.0)
                nc.scalar.activation(out=env[:, 2, part], in_=z3[:, 0:half], func=ACT.Square, bias=-0.5, scale=1.0)
                if 1 <= ch <= W_CHUNKS:
                    w1 = zpsum.tile([P, N_MOVING], F32, tag="w%d" % c)
                    banks.append(w1)
                    nc.tensor.matmul(out=w1[:, 0:half], lhsT=per_step[:], rhs=xg[:, part], start=True, stop=False)
                    for r in range(3):
                        nc.tensor.matmul(out=w1[:, 0:half], lhsT=minus1[:], rhs=sb[:, r, part], start=False, stop=(r == 2))
            nc.scalar.activation(out=env[:, 0, :], in_=dist[:], func=ACT.Square, bias=1.5, scale=-1.0)
            if 1 <= ch <= W_CHUNKS:
                for c in range(PASSES):
                    part = slice(c * half, (c + 1) * half)
                    nc.scalar.activation(out=dist[:, part], in_=banks[c][:, 0:half], func=ACT.Square, bias=-ROOT2, scale=ROOT2)
            else:
                nc.scalar.activation(out=dist[:], in_=dist[:], func=ACT.Abs, bias=-0.5, scale=1.0)
                nc.scalar.activation(out=dist[:], in_=dist[:], func=ACT.Square, bias=-ROOT2 / 2.0, scale=ROOT2)
            cap = deep.tile([P, size], BF16, tag="cap")
            if ch < HEAD_ON_VECTOR:
                nc.vector.tensor_scalar(out=cap[:], in0=dist[:], scalar1=-1.0, scalar2=1.5, op0=ALU.mult, op1=ALU.add)
            else:
                nc.scalar.activation(out=cap[:], in_=dist[:], func=ACT.Identity, bias=1.5, scale=-1.0)
            state[ch] = {"sb": sb, "env": env, "cap": cap, "size": size}

        def stage_x(ch):
            st = state[ch]
            size = st["size"]
            lanes = PASSES * CHUNKS[ch][0]
            plane = size // lanes
            slab = slabs[ch % SLABS]
            planes = slab[:, 0:lanes, 0 : BASES * plane].rearrange("p a (k e) -> p k a e", k=BASES)
            env = st["env"]
            nc.vector.tensor_tensor(
                out=env[:], in0=env[:], in1=st["cap"][:].unsqueeze(1).to_broadcast([P, 3, size]), op=ALU.min
            )
            mask = two.tile([P, BASES, size], BF16, tag="mask")
            for m in range(0, BASES, 3):
                classes = min(3, BASES - m)
                nc.vector.tensor_scalar(
                    out=mask[:, m : m + classes, :], in0=st["sb"][:, 0:classes, :], scalar1=float(m // 3 - 2), scalar2=0.5,
                    op0=ALU.is_equal, op1=ALU.mult,
                )
            for r in range(3):
                slots = len(range(r, BASES, 3))
                nc.vector.tensor_tensor(
                    out=planes[:, r:BASES:3, :, :],
                    in0=mask[:, r:BASES:3, :].rearrange("p m (a e) -> p m a e", a=lanes),
                    in1=env[:, r, :].rearrange("p (a e) -> p a e", a=lanes).unsqueeze(1).to_broadcast([P, slots, lanes, plane]),
                    op=ALU.mult,
                )

        def stage_q(ch, g):
            slab = slabs[ch % SLABS]
            groups = CHUNKS[ch][0]
            if g == 0:
                codes = deep.tile([P, PASSES, groups * N_MOVING], U32, tag="codes", align_bytes=64)
                scales = deep.tile([P, PASSES, groups * N_MOVING], U8, tag="scales", align_bytes=64)
                state[ch]["codes"] = codes
                state[ch]["scales"] = scales
            cols = slice(g * N_MOVING, (g + 1) * N_MOVING)
            for c in range(PASSES):
                nc.vector.quantize_mx(
                    out=state[ch]["codes"][:, c, cols].bitcast(E4X4),
                    scales=state[ch]["scales"][:, c, cols],
                    in_=slab[:, c * groups + g, :],
                )

        def stage_out(ch, g):
            ni = CHUNKS[ch][1]
            width = ni * BASES
            cols = slice(g * N_MOVING, (g + 1) * N_MOVING)
            lo = starts[ch] + g * ni
            for ot in range(OUTS // P):
                rows = slice(ot * P, (ot + 1) * P)
                acc = psum.tile([P, N_MOVING], F32, tag="acc")
                for c in range(PASSES):
                    nc.tensor.matmul_mx(
                        out=acc[:],
                        lhsT=g_codes[:, c, rows].bitcast(E5X4),
                        lhsT_scale=g_scales[:, c, rows],
                        rhs=state[ch]["codes"][:, c, cols].bitcast(E4X4),
                        rhs_scale=state[ch]["scales"][:, c, cols],
                        start=(c == 0),
                        stop=(c == PASSES - 1),
                    )
                stage = outp.tile([P, width], F32, tag="stage")
                nc.scalar.activation(
                    out=stage[:].rearrange("p (i k) -> p i k", k=BASES),
                    in_=acc[:, 0:width].rearrange("p (k i) -> p i k", k=BASES),
                    func=ACT.Copy,
                    scale=ws[:, 0:1],
                )
                nc.sync.dma_start(out=out[rows, lo : lo + ni, :].rearrange("o i k -> o (i k)"), in_=stage[:])

        n_chunks = len(CHUNKS)
        stage_a(0)
        for c in range(PASSES):
            nc.vector.tensor_copy(
                out=g_grouped[:, c].rearrange("p (n i) j -> p n j i", i=PACK),
                in_=g_raw[:, c].rearrange("p j (n i) -> p n j i", i=PACK),
            )
        for ch in range(1, AHEAD):
            stage_a(ch)
        for c in range(PASSES):
            nc.vector.quantize_mx(
                out=g_codes[:, c, :].bitcast(E5X4),
                scales=g_scales[:, c, :],
                in_=g_grouped[:, c].rearrange("p o j -> p (o j)"),
            )
        for ch in range(n_chunks):
            stage_x(ch)
            if ch + AHEAD < n_chunks:
                stage_a(ch + AHEAD)
            for g in range(CHUNKS[ch][0]):
                stage_q(ch, g)
                stage_out(ch, g)
